import numpy as np
import ml_dtypes


def mxq(x, axis, fmt="e4m3"):
    dtype, down = {"e4m3": (ml_dtypes.float8_e4m3fn, 7), "e5m2": (ml_dtypes.float8_e5m2, 14)}[fmt]
    v = np.moveaxis(np.asarray(x, np.float32).astype(ml_dtypes.bfloat16).astype(np.float64), axis, -1)
    blocks = v.reshape(v.shape[:-1] + (-1, 32))
    amax = np.abs(blocks).max(-1, keepdims=True)
    byte = np.maximum(np.where(amax > 0, np.frexp(amax)[1] - 1 + 127, 0) - down, 1)
    scale = np.exp2(byte - 127.0)
    codes = (blocks / scale).astype(np.float32).astype(dtype).astype(np.float64)
    return np.moveaxis((codes * scale).reshape(v.shape), -1, axis)


WIDE = False


def mx_kscale(k):
    if not WIDE:
        return np.ones(k)
    levels = np.array([10, -10, 5, -5, 0])
    a = np.random.permutation(np.resize(levels, k // 512 * 4)).reshape(k // 512, 4)
    idx = np.arange(k)
    return np.exp2(a[idx // 512, idx % 128 // 32])


BF16 = ml_dtypes.bfloat16


def bf(x):
    return np.asarray(x, np.float32).astype(BF16)


def f64(x):
    return np.asarray(x).astype(np.float64)


E2M1 = np.array([0.0, 0.5, 1.0, 1.5, 2.0, 3.0, 4.0, 6.0, -0.0, -0.5, -1.0, -1.5, -2.0, -3.0, -4.0, -6.0])


def pack_weight(w, fmt):
    k, n = w.shape
    w = f64(bf(w)).reshape(k // 32, 32, n)
    amax = np.abs(w).max(1)
    if fmt == "e4m3":
        byte = np.frexp(amax)[1] - 1 + 127 - 7
    else:
        mant, ex = np.frexp(amax / 6.0)
        byte = np.where(mant > 0.5, ex, ex - 1) + 127
    byte = np.clip(np.where(amax > 0, byte, 1), 1, 254)
    scaled = (w * np.exp2(127.0 - byte)[:, None, :]).reshape(k, n).astype(np.float32)
    by_word = np.ascontiguousarray(scaled.reshape(k // 512, 128, 4, n).transpose(0, 1, 3, 2))
    if fmt == "e4m3":
        words = by_word.astype(ml_dtypes.float8_e4m3fn).view(np.uint8)
    else:
        c = by_word.astype(ml_dtypes.float4_e2m1fn).view(np.uint8) & 0xF
        words = c[..., 0::2] | (c[..., 1::2] << 4)
    return np.ascontiguousarray(words), np.ascontiguousarray(byte.astype(np.uint8).reshape(k // 512, 16, n))


def unpack_weight(words, scales, fmt):
    g, p, n, _ = words.shape
    if fmt == "e4m3":
        vals = np.ascontiguousarray(words).view(ml_dtypes.float8_e4m3fn).astype(np.float64)
    else:
        nib = np.empty((g, p, n, 4), np.uint8)
        nib[..., 0::2] = words & 0xF
        nib[..., 1::2] = words >> 4
        vals = E2M1[nib]
    vals = vals * np.repeat(np.exp2(scales.astype(np.float64) - 127.0), 8, axis=1)[..., None]
    return vals.transpose(0, 1, 3, 2).reshape(g * 512, n)


G, GI, GO, B = 32, 128, 128, 128
K = G * GI
N = G * GO


def build_mask():
    mask = np.ones((N, K))
    for g in range(G):
        mask[g * GO:(g + 1) * GO, g * GI:(g + 1) * GI] = 0.0
    return mask


def setup_inputs():
    s = mx_kscale(K)
    bound = 1.0 / np.sqrt(K)
    W = np.random.uniform(-bound, bound, (N, K)) * build_mask()
    data = bf(np.random.standard_normal((B, K)) * s)
    words, scales = pack_weight((W / s[None, :]).T, "e4m3")
    return {"data": data,
            "W_words": words,
            "W_scales": scales,
            "b": bf(np.random.standard_normal(N) * 0.3)}


def reference(data, W_words, W_scales, b):
    return (mxq(f64(data), 1, "e4m3") @ unpack_weight(W_words, W_scales, "e4m3")) + f64(b)

@@ -1,0 +1,138 @@
+from contextlib import ExitStack
+
+import concourse.mybir as mybir
+from concourse.masks import make_identity
+
+F32 = mybir.dt.float32
+BF16 = mybir.dt.bfloat16
+I32 = mybir.dt.int32
+U32 = mybir.dt.uint32
+U8 = mybir.dt.uint8
+FP8X4 = mybir.dt.float8_e4m3fn_x4
+ADD = mybir.AluOpType.add
+
+P = 128
+B = 128
+K = 4096
+N = 4096
+PASSES = K // 512
+NT = 512
+BANKS = N // NT
+PIECE = 1024
+FLOPS = 2 * B * K * N
+
+
+def tile_groupfc_w_kernel(tc, data, W_words, W_scales, b, out):
+    nc = tc.nc
+    with ExitStack() as ctx:
+        ctx.enter_context(tc.manual_schedule())
+        keep = ctx.enter_context(tc.tile_pool(name="keep", bufs=1))
+        psum = ctx.enter_context(tc.psum_pool(name="psum", bufs=1))
+
+        planes = [keep.tile([P, N], U8, name="planes%d" % h, align_bytes=64) for h in range(2)]
+        b_rows = keep.tile([P, NT], BF16, name="b_rows")
+        ident_f = keep.tile([P, P], F32, name="ident_f")
+        ident_b = keep.tile([P, P], BF16, name="ident_b")
+        x_sb = keep.tile([P, K], BF16, name="x_sb")
+        grouped = [keep.tile([P, 1024], BF16, name="grouped%d" % i, align_bytes=64) for i in range(4)]
+        x_codes = keep.tile([P, PASSES * B], U32, name="x_codes", align_bytes=64)
+        x_scales = keep.tile([P, PASSES * B], U8, name="x_scales", align_bytes=64)
+        w_full = [keep.tile([P, N], U32, name="w%d" % g, align_bytes=64) for g in range(PASSES - 1)]
+        w_last = [keep.tile([P, PIECE], U32, name="wl%d" % i, align_bytes=64) for i in range(N // PIECE)]
+        res = [keep.tile([P, PIECE], F32, name="res%d" % i) for i in range(N // PIECE)]
+
+        for h in range(2):
+            nc.vector.memset(planes[h][:].bitcast(I32), 0)
+        nc.vector.memset(b_rows[:], 0.0)
+        make_identity(nc, ident_b[:])
+        make_identity(nc, ident_f[:])
+
+        nc.sync.dma_start(out=x_sb[:], in_=data)
+        nc.scalar.dma_start(out=b_rows[0:BANKS, :], in_=b.rearrange("(c n) -> c n", c=BANKS))
+        for h in range(2):
+            for q in range(4):
+                nc.sync.dma_start(
+                    out=planes[h][32 * q : 32 * q + 16, :].bitcast(I32),
+                    in_=W_scales[4 * h : 4 * h + 4, 4 * q : 4 * q + 4, :].bitcast(I32),
+                )
+        for g in range(PASSES - 1):
+            nc.sync.dma_start(
+                out=w_full[g][:].bitcast(I32),
+                in_=W_words[g].rearrange("p n t -> p (n t)").bitcast(I32),
+            )
+        last_rows = W_words[PASSES - 1].rearrange("p n t -> p (n t)")
+        for i in range(N // PIECE):
+            nc.sync.dma_start(
+                out=w_last[i][:].bitcast(I32),
+                in_=last_rows[:, 4 * PIECE * i : 4 * PIECE * (i + 1)].bitcast(I32),
+            )
+
+        def res_cols(c):
+            per = PIECE // NT
+            return res[c // per][:, NT * (c % per) : NT * (c % per + 1)]
+
+        def bias_tile(c):
+            spread = psum.tile([P, NT], F32, name="spread%d" % c, tag="bank%d" % (4 + c % 4))
+            nc.tensor.matmul(
+                out=spread[:],
+                lhsT=ident_b[:, c : c + 1].to_broadcast([P, P]),
+                rhs=b_rows[:],
+                start=True,
+                stop=True,
+            )
+            if c % 2 == 0:
+                nc.vector.tensor_copy(out=res_cols(c), in_=spread[:])
+            else:
+                nc.scalar.copy(out=res_cols(c), in_=spread[:])
+
+        for c in range(4):
+            bias_tile(c)
+
+        x_words = x_sb[:].bitcast(F32)
+        for i in range(4):
+            xt = psum.tile([P, 2, 2, B], F32, name="xt%d" % i, tag="bank%d" % i)
+            for gi in range(2):
+                g = 2 * i + gi
+                for u in range(2):
+                    nc.tensor.transpose(xt[:, gi, u, :], x_words[:, 256 * g + u : 256 * (g + 1) : 2], ident_f[:])
+            dst = grouped[i][:].bitcast(F32).rearrange("p (g r u) -> p g r u", g=2, u=2)
+            src = xt[:].rearrange("p g u r -> p g r u")
+            if i % 2 == 0:
+                nc.vector.tensor_copy(out=dst, in_=src)
+            else:
+                nc.scalar.copy(out=dst, in_=src)
+        for i in range(4):
+            nc.vector.quantize_mx(
+                out=x_codes[:, 256 * i : 256 * (i + 1)].bitcast(FP8X4),
+                scales=x_scales[:, 256 * i : 256 * (i + 1)],
+                in_=grouped[i][:],
+            )
+
+        for c in range(4, BANKS):
+            bias_tile(c)
+
+        acc = [psum.tile([P, NT], F32, name="acc%d" % c, tag="bank%d" % c) for c in range(BANKS)]
+        for g in range(PASSES):
+            off = 4 * (g % 4)
+            for c in range(BANKS):
+                if g < PASSES - 1:
+                    w_cols = w_full[g][:, NT * c : NT * (c + 1)]
+                else:
+                    per = PIECE // NT
+                    w_cols = w_last[c // per][:, NT * (c % per) : NT * (c % per + 1)]
+                nc.tensor.matmul_mx(
+                    out=acc[c][:],
+                    lhsT=x_codes[:, B * g : B * (g + 1)].bitcast(FP8X4),
+                    lhsT_scale=x_scales[:, B * g : B * (g + 1)],
+                    rhs=w_cols.bitcast(FP8X4),
+                    rhs_scale=planes[g // 4][off:P, NT * c : NT * (c + 1)],
+                    start=(g == 0),
+                    stop=(g == PASSES - 1),
+                )
+
+        for c in range(BANKS):
+            nc.vector.tensor_tensor(out=res_cols(c), in0=acc[c][:], in1=res_cols(c), op=ADD)
+            per = PIECE // NT
+            if c % per == per - 1:
+                i = c // per
+                nc.sync.dma_start(out=out[:, PIECE * i : PIECE * (i + 1)], in_=res[i][:])

@@ -50,10 +50,10 @@ def tile_groupfc_w_kernel(tc, data, W_words, W_scales, b, out):
         nc.sync.dma_start(out=x_sb[:], in_=data)
         nc.scalar.dma_start(out=b_rows[0:BANKS, :], in_=b.rearrange("(c n) -> c n", c=BANKS))
         for h in range(2):
-            for q in range(4):
-                nc.sync.dma_start(
-                    out=planes[h][32 * q : 32 * q + 16, :].bitcast(I32),
-                    in_=W_scales[4 * h : 4 * h + 4, 4 * q : 4 * q + 4, :].bitcast(I32),
+            for q in (0, 2, 1, 3):
+                nc.gpsimd.dma_start(
+                    out=planes[h][32 * q : 32 * q + 16, :].bitcast(F32),
+                    in_=W_scales[4 * h : 4 * h + 4, 4 * q : 4 * q + 4, :].bitcast(F32),
                 )
         for g in range(PASSES - 1):
             nc.sync.dma_start(

@@ -18,8 +18,12 @@ N = 4096
 PASSES = K // 512
 NT = 512
 BANKS = N // NT
-PIECE = 1024
 FLOPS = 2 * B * K * N
+
+PLAN = [(g, 0, 8) for g in range(5)] + [
+    (5, 0, 4), (6, 0, 4), (7, 0, 4), (5, 4, 8), (6, 4, 8), (7, 4, 5), (7, 5, 6), (7, 6, 7), (7, 7, 8),
+]
+STORES = [(0, 2), (2, 4), (4, 5), (5, 6), (6, 7), (7, 8)]
 
 
 def tile_groupfc_w_kernel(tc, data, W_words, W_scales, b, out):
@@ -37,9 +41,10 @@ def tile_groupfc_w_kernel(tc, data, W_words, W_scales, b, out):
         grouped = [keep.tile([P, 1024], BF16, name="grouped%d" % i, align_bytes=64) for i in range(4)]
         x_codes = keep.tile([P, PASSES * B], U32, name="x_codes", align_bytes=64)
         x_scales = keep.tile([P, PASSES * B], U8, name="x_scales", align_bytes=64)
-        w_full = [keep.tile([P, N], U32, name="w%d" % g, align_bytes=64) for g in range(PASSES - 1)]
-        w_last = [keep.tile([P, PIECE], U32, name="wl%d" % i, align_bytes=64) for i in range(N // PIECE)]
-        res = [keep.tile([P, PIECE], F32, name="res%d" % i) for i in range(N // PIECE)]
+        w_tiles = [
+            keep.tile([P, NT * (c1 - c0)], U32, name="w%d_%d" % (g, c0), align_bytes=64) for g, c0, c1 in PLAN
+        ]
+        res = [keep.tile([P, NT * (c1 - c0)], F32, name="res%d" % c0) for c0, c1 in STORES]
 
         for h in range(2):
             nc.vector.memset(planes[h][:].bitcast(I32), 0)
@@ -50,26 +55,22 @@ def tile_groupfc_w_kernel(tc, data, W_words, W_scales, b, out):
         nc.sync.dma_start(out=x_sb[:], in_=data)
         nc.scalar.dma_start(out=b_rows[0:BANKS, :], in_=b.rearrange("(c n) -> c n", c=BANKS))
         for h in range(2):
-            for q in (0, 2, 1, 3):
-                nc.gpsimd.dma_start(
-                    out=planes[h][32 * q : 32 * q + 16, :].bitcast(F32),
-                    in_=W_scales[4 * h : 4 * h + 4, 4 * q : 4 * q + 4, :].bitcast(F32),
+            for q in range(4):
+                nc.sync.dma_start(
+                    out=planes[h][32 * q : 32 * q + 16, :].bitcast(I32),
+                    in_=W_scales[4 * h : 4 * h + 4, 4 * q : 4 * q + 4, :].bitcast(I32),
                 )
-        for g in range(PASSES - 1):
+        for w_tile, (g, c0, c1) in zip(w_tiles, PLAN):
             nc.sync.dma_start(
-                out=w_full[g][:].bitcast(I32),
-                in_=W_words[g].rearrange("p n t -> p (n t)").bitcast(I32),
-            )
-        last_rows = W_words[PASSES - 1].rearrange("p n t -> p (n t)")
-        for i in range(N // PIECE):
-            nc.sync.dma_start(
-                out=w_last[i][:].bitcast(I32),
-                in_=last_rows[:, 4 * PIECE * i : 4 * PIECE * (i + 1)].bitcast(I32),
+                out=w_tile[:].bitcast(I32),
+                in_=W_words[g].rearrange("p n t -> p (n t)")[:, 4 * NT * c0 : 4 * NT * c1].bitcast(I32),
             )
 
         def res_cols(c):
-            per = PIECE // NT
-            return res[c // per][:, NT * (c % per) : NT * (c % per + 1)]
+            for r, (c0, c1) in zip(res, STORES):
+                if c0 <= c < c1:
+                    return r[:, NT * (c - c0) : NT * (c - c0 + 1)]
+            raise ValueError("no store holds bank %d" % c)
 
         def bias_tile(c):
             spread = psum.tile([P, NT], F32, name="spread%d" % c, tag="bank%d" % (4 + c % 4))
@@ -112,27 +113,21 @@ def tile_groupfc_w_kernel(tc, data, W_words, W_scales, b, out):
             bias_tile(c)
 
         acc = [psum.tile([P, NT], F32, name="acc%d" % c, tag="bank%d" % c) for c in range(BANKS)]
-        for g in range(PASSES):
+        for w_tile, (g, c0, c1) in zip(w_tiles, PLAN):
             off = 4 * (g % 4)
-            for c in range(BANKS):
-                if g < PASSES - 1:
-                    w_cols = w_full[g][:, NT * c : NT * (c + 1)]
-                else:
-                    per = PIECE // NT
-                    w_cols = w_last[c // per][:, NT * (c % per) : NT * (c % per + 1)]
+            for c in range(c0, c1):
                 nc.tensor.matmul_mx(
                     out=acc[c][:],
                     lhsT=x_codes[:, B * g : B * (g + 1)].bitcast(FP8X4),
                     lhsT_scale=x_scales[:, B * g : B * (g + 1)],
-                    rhs=w_cols.bitcast(FP8X4),
+                    rhs=w_tile[:, NT * (c - c0) : NT * (c - c0 + 1)].bitcast(FP8X4),
                     rhs_scale=planes[g // 4][off:P, NT * c : NT * (c + 1)],
                     start=(g == 0),
                     stop=(g == PASSES - 1),
                 )
-
-        for c in range(BANKS):
-            nc.vector.tensor_tensor(out=res_cols(c), in0=acc[c][:], in1=res_cols(c), op=ADD)
-            per = PIECE // NT
-            if c % per == per - 1:
-                i = c // per
-                nc.sync.dma_start(out=out[:, PIECE * i : PIECE * (i + 1)], in_=res[i][:])
+            if g == PASSES - 1:
+                for c in range(c0, c1):
+                    nc.vector.tensor_tensor(out=res_cols(c), in0=acc[c][:], in1=res_cols(c), op=ADD)
+                    for r, (s0, s1) in zip(res, STORES):
+                        if s1 == c + 1:
+                            nc.sync.dma_start(out=out[:, NT * s0 : NT * s1], in_=r[:])

@@ -54,12 +54,11 @@ def tile_groupfc_w_kernel(tc, data, W_words, W_scales, b, out):
 
         nc.sync.dma_start(out=x_sb[:], in_=data)
         nc.scalar.dma_start(out=b_rows[0:BANKS, :], in_=b.rearrange("(c n) -> c n", c=BANKS))
-        for h in range(2):
-            for q in range(4):
-                nc.sync.dma_start(
-                    out=planes[h][32 * q : 32 * q + 16, :].bitcast(I32),
-                    in_=W_scales[4 * h : 4 * h + 4, 4 * q : 4 * q + 4, :].bitcast(I32),
-                )
+        for h, q in ((0, 2), (0, 3), (1, 2), (1, 3), (0, 0), (0, 1), (1, 0), (1, 1)):
+            nc.sync.dma_start(
+                out=planes[h][32 * q : 32 * q + 16, :].bitcast(I32),
+                in_=W_scales[4 * h : 4 * h + 4, 4 * q : 4 * q + 4, :].bitcast(I32),
+            )
         for w_tile, (g, c0, c1) in zip(w_tiles, PLAN):
             nc.sync.dma_start(
                 out=w_tile[:].bitcast(I32),

@@ -53,7 +53,7 @@ def tile_groupfc_w_kernel(tc, data, W_words, W_scales, b, out):
         make_identity(nc, ident_f[:])
 
         nc.sync.dma_start(out=x_sb[:], in_=data)
-        nc.scalar.dma_start(out=b_rows[0:BANKS, :], in_=b.rearrange("(c n) -> c n", c=BANKS))
+        nc.sync.dma_start(out=b_rows[0:BANKS, :], in_=b.rearrange("(c n) -> c n", c=BANKS))
         for h, q in ((0, 2), (0, 3), (1, 2), (1, 3), (0, 0), (0, 1), (1, 0), (1, 1)):
             nc.sync.dma_start(
                 out=planes[h][32 * q : 32 * q + 16, :].bitcast(I32),
@@ -80,10 +80,7 @@ def tile_groupfc_w_kernel(tc, data, W_words, W_scales, b, out):
                 start=True,
                 stop=True,
             )
-            if c % 2 == 0:
-                nc.vector.tensor_copy(out=res_cols(c), in_=spread[:])
-            else:
-                nc.scalar.copy(out=res_cols(c), in_=spread[:])
+            nc.vector.tensor_copy(out=res_cols(c), in_=spread[:])
 
         for c in range(4):
             bias_tile(c)
@@ -97,10 +94,7 @@ def tile_groupfc_w_kernel(tc, data, W_words, W_scales, b, out):
                     nc.tensor.transpose(xt[:, gi, u, :], x_words[:, 256 * g + u : 256 * (g + 1) : 2], ident_f[:])
             dst = grouped[i][:].bitcast(F32).rearrange("p (g r u) -> p g r u", g=2, u=2)
             src = xt[:].rearrange("p g u r -> p g r u")
-            if i % 2 == 0:
-                nc.vector.tensor_copy(out=dst, in_=src)
-            else:
-                nc.scalar.copy(out=dst, in_=src)
+            nc.vector.tensor_copy(out=dst, in_=src)
         for i in range(4):
             nc.vector.quantize_mx(
                 out=x_codes[:, 256 * i : 256 * (i + 1)].bitcast(FP8X4),

@@ -29,7 +29,6 @@ STORES = [(0, 2), (2, 4), (4, 5), (5, 6), (6, 7), (7, 8)]
 def tile_groupfc_w_kernel(tc, data, W_words, W_scales, b, out):
     nc = tc.nc
     with ExitStack() as ctx:
-        ctx.enter_context(tc.manual_schedule())
         keep = ctx.enter_context(tc.tile_pool(name="keep", bufs=1))
         psum = ctx.enter_context(tc.psum_pool(name="psum", bufs=1))
 

@@ -20,8 +20,8 @@ NT = 512
 BANKS = N // NT
 FLOPS = 2 * B * K * N
 
-PLAN = [(g, 0, 8) for g in range(5)] + [
-    (5, 0, 4), (6, 0, 4), (7, 0, 4), (5, 4, 8), (6, 4, 8), (7, 4, 5), (7, 5, 6), (7, 6, 7), (7, 7, 8),
+PLAN = [(g, 0, 8) for g in range(6)] + [
+    (6, 0, 4), (7, 0, 4), (6, 4, 8), (7, 4, 5), (7, 5, 6), (7, 6, 7), (7, 7, 8),
 ]
 STORES = [(0, 2), (2, 4), (4, 5), (5, 6), (6, 7), (7, 8)]
 

from contextlib import ExitStack

import concourse.mybir as mybir
from concourse.masks import make_identity

F32 = mybir.dt.float32
BF16 = mybir.dt.bfloat16
I32 = mybir.dt.int32
U32 = mybir.dt.uint32
U8 = mybir.dt.uint8
FP8X4 = mybir.dt.float8_e4m3fn_x4
ADD = mybir.AluOpType.add

P = 128
B = 128
K = 4096
N = 4096
PASSES = K // 512
NT = 512
BANKS = N // NT
FLOPS = 2 * B * K * N

PLAN = [(g, 0, 8) for g in range(6)] + [
    (6, 0, 4), (7, 0, 4), (6, 4, 8), (7, 4, 5), (7, 5, 6), (7, 6, 7), (7, 7, 8),
]
STORES = [(0, 2), (2, 4), (4, 5), (5, 6), (6, 7), (7, 8)]


def tile_groupfc_w_kernel(tc, data, W_words, W_scales, b, out):
    nc = tc.nc
    with ExitStack() as ctx:
        keep = ctx.enter_context(tc.tile_pool(name="keep", bufs=1))
        psum = ctx.enter_context(tc.psum_pool(name="psum", bufs=1))

        planes = [keep.tile([P, N], U8, name="planes%d" % h, align_bytes=64) for h in range(2)]
        b_rows = keep.tile([P, NT], BF16, name="b_rows")
        ident_f = keep.tile([P, P], F32, name="ident_f")
        ident_b = keep.tile([P, P], BF16, name="ident_b")
        x_sb = keep.tile([P, K], BF16, name="x_sb")
        grouped = [keep.tile([P, 1024], BF16, name="grouped%d" % i, align_bytes=64) for i in range(4)]
        x_codes = keep.tile([P, PASSES * B], U32, name="x_codes", align_bytes=64)
        x_scales = keep.tile([P, PASSES * B], U8, name="x_scales", align_bytes=64)
        w_tiles = [
            keep.tile([P, NT * (c1 - c0)], U32, name="w%d_%d" % (g, c0), align_bytes=64) for g, c0, c1 in PLAN
        ]
        res = [keep.tile([P, NT * (c1 - c0)], F32, name="res%d" % c0) for c0, c1 in STORES]

        for h in range(2):
            nc.vector.memset(planes[h][:].bitcast(I32), 0)
        nc.vector.memset(b_rows[:], 0.0)
        make_identity(nc, ident_b[:])
        make_identity(nc, ident_f[:])

        nc.sync.dma_start(out=x_sb[:], in_=data)
        nc.sync.dma_start(out=b_rows[0:BANKS, :], in_=b.rearrange("(c n) -> c n", c=BANKS))
        for h, q in ((0, 2), (0, 3), (1, 2), (1, 3), (0, 0), (0, 1), (1, 0), (1, 1)):
            nc.sync.dma_start(
                out=planes[h][32 * q : 32 * q + 16, :].bitcast(I32),
                in_=W_scales[4 * h : 4 * h + 4, 4 * q : 4 * q + 4, :].bitcast(I32),
            )
        for w_tile, (g, c0, c1) in zip(w_tiles, PLAN):
            nc.sync.dma_start(
                out=w_tile[:].bitcast(I32),
                in_=W_words[g].rearrange("p n t -> p (n t)")[:, 4 * NT * c0 : 4 * NT * c1].bitcast(I32),
            )

        def res_cols(c):
            for r, (c0, c1) in zip(res, STORES):
                if c0 <= c < c1:
                    return r[:, NT * (c - c0) : NT * (c - c0 + 1)]
            raise ValueError("no store holds bank %d" % c)

        def bias_tile(c):
            spread = psum.tile([P, NT], F32, name="spread%d" % c, tag="bank%d" % (4 + c % 4))
            nc.tensor.matmul(
                out=spread[:],
                lhsT=ident_b[:, c : c + 1].to_broadcast([P, P]),
                rhs=b_rows[:],
                start=True,
                stop=True,
            )
            nc.vector.tensor_copy(out=res_cols(c), in_=spread[:])

        for c in range(4):
            bias_tile(c)

        x_words = x_sb[:].bitcast(F32)
        for i in range(4):
            xt = psum.tile([P, 2, 2, B], F32, name="xt%d" % i, tag="bank%d" % i)
            for gi in range(2):
                g = 2 * i + gi
                for u in range(2):
                    nc.tensor.transpose(xt[:, gi, u, :], x_words[:, 256 * g + u : 256 * (g + 1) : 2], ident_f[:])
            dst = grouped[i][:].bitcast(F32).rearrange("p (g r u) -> p g r u", g=2, u=2)
            src = xt[:].rearrange("p g u r -> p g r u")
            nc.vector.tensor_copy(out=dst, in_=src)
        for i in range(4):
            nc.vector.quantize_mx(
                out=x_codes[:, 256 * i : 256 * (i + 1)].bitcast(FP8X4),
                scales=x_scales[:, 256 * i : 256 * (i + 1)],
                in_=grouped[i][:],
            )

        for c in range(4, BANKS):
            bias_tile(c)

        acc = [psum.tile([P, NT], F32, name="acc%d" % c, tag="bank%d" % c) for c in range(BANKS)]
        for w_tile, (g, c0, c1) in zip(w_tiles, PLAN):
            off = 4 * (g % 4)
            for c in range(c0, c1):
                nc.tensor.matmul_mx(
                    out=acc[c][:],
                    lhsT=x_codes[:, B * g : B * (g + 1)].bitcast(FP8X4),
                    lhsT_scale=x_scales[:, B * g : B * (g + 1)],
                    rhs=w_tile[:, NT * (c - c0) : NT * (c - c0 + 1)].bitcast(FP8X4),
                    rhs_scale=planes[g // 4][off:P, NT * c : NT * (c + 1)],
                    start=(g == 0),
                    stop=(g == PASSES - 1),
                )
            if g == PASSES - 1:
                for c in range(c0, c1):
                    nc.vector.tensor_tensor(out=res_cols(c), in0=acc[c][:], in1=res_cols(c), op=ADD)
                    for r, (s0, s1) in zip(res, STORES):
                        if s1 == c + 1:
                            nc.sync.dma_start(out=out[:, NT * s0 : NT * s1], in_=r[:])
